import numpy as np
import ml_dtypes


def mxq(x, axis, fmt="e4m3"):
    dtype, down = {"e4m3": (ml_dtypes.float8_e4m3fn, 7), "e5m2": (ml_dtypes.float8_e5m2, 14)}[fmt]
    v = np.moveaxis(np.asarray(x, np.float32).astype(ml_dtypes.bfloat16).astype(np.float64), axis, -1)
    blocks = v.reshape(v.shape[:-1] + (-1, 32))
    amax = np.abs(blocks).max(-1, keepdims=True)
    byte = np.maximum(np.where(amax > 0, np.frexp(amax)[1] - 1 + 127, 0) - down, 1)
    scale = np.exp2(byte - 127.0)
    codes = (blocks / scale).astype(np.float32).astype(dtype).astype(np.float64)
    return np.moveaxis((codes * scale).reshape(v.shape), -1, axis)


WIDE = False


def mx_kscale(k):
    if not WIDE:
        return np.ones(k)
    levels = np.array([10, -10, 5, -5, 0])
    a = np.random.permutation(np.resize(levels, k // 512 * 4)).reshape(k // 512, 4)
    idx = np.arange(k)
    return np.exp2(a[idx // 512, idx % 128 // 32])


BF16 = ml_dtypes.bfloat16


def bf(x):
    return np.asarray(x, np.float32).astype(BF16)


def f64(x):
    return np.asarray(x).astype(np.float64)


B, NQ = 4096, 10
CONTROL = 0
DIM = 1 << NQ
HALF = DIM // 2


def setup_inputs():
    on = np.nonzero((np.arange(DIM) & (1 << (NQ - CONTROL - 1))) != 0)[0]
    sv = np.ones(DIM)
    sv[on] = mx_kscale(HALF)
    return {"state": bf(np.random.standard_normal((B, DIM)) * sv),
            "target_matrix": bf(np.random.standard_normal((DIM, DIM)) / np.sqrt(HALF) / sv[:, None]),
            "control": CONTROL,
            "num_qubits": NQ}


def reference(state, target_matrix, control, num_qubits):
    dim = 1 << num_qubits
    mask = 1 << (num_qubits - control - 1)
    c1_mask = (np.arange(dim) & mask) != 0
    on = np.nonzero(c1_mask)[0]
    st, tm = f64(state), f64(target_matrix)
    transformed = mxq(st[:, on], 1, "e4m3") @ mxq(tm[np.ix_(on, on)], 0, "e4m3")
    out = st.copy()
    out[:, on] = transformed
    return out

@@ -1,0 +1,133 @@
+from contextlib import ExitStack
+
+import concourse.mybir as mybir
+from concourse.masks import make_identity
+
+BF16 = mybir.dt.bfloat16
+F32 = mybir.dt.float32
+U32 = mybir.dt.uint32
+U8 = mybir.dt.uint8
+FP8X4 = mybir.dt.float8_e4m3fn_x4
+
+P = 128
+PACK = 4
+BATCH = 4096
+DIM = 1024
+HALF = DIM // 2
+PAIR = 2
+WORD_HALVES = 2
+BANK_F32 = 512
+
+ROW_GROUPS = BATCH // P
+CHUNK = 4
+CHUNKS = ROW_GROUPS // CHUNK
+GROUPS_PER_BANK = BANK_F32 // (WORD_HALVES * P)
+BANKS_PER_CHUNK = CHUNK // GROUPS_PER_BANK
+
+WORD_BANKS = 2 * BANKS_PER_CHUNK
+PROD_BANKS = 8 - WORD_BANKS
+OUT_BUFS = 4
+STAGE_BUFS = 3
+
+FLOPS = 2 * BATCH * HALF * HALF
+BYTES = BATCH * DIM * 2 + HALF * HALF * 2 + BATCH * DIM * 4
+
+
+def tile_builtcontrolled_t_kernel(tc, state, target_matrix, control, num_qubits, out):
+    nc = tc.nc
+    assert control == 0 and num_qubits == 10
+    assert tuple(state.shape) == (BATCH, DIM) and tuple(target_matrix.shape) == (DIM, DIM)
+
+    state_rows = state.rearrange("(p t) d -> p t d", t=ROW_GROUPS)
+    out_rows = out.rearrange("(p t) d -> p t d", t=ROW_GROUPS)
+
+    with ExitStack() as ctx:
+        const = ctx.enter_context(tc.tile_pool(name="const", bufs=1))
+        resident = ctx.enter_context(tc.tile_pool(name="resident", bufs=CHUNKS))
+        stage = ctx.enter_context(tc.tile_pool(name="stage", bufs=STAGE_BUFS))
+        results = ctx.enter_context(tc.tile_pool(name="results", bufs=OUT_BUFS))
+        psum_words = ctx.enter_context(tc.psum_pool(name="psum_words", bufs=WORD_BANKS))
+        psum_prod = ctx.enter_context(tc.psum_pool(name="psum_prod", bufs=PROD_BANKS))
+
+        w_rows = const.tile([P, PACK, HALF], BF16)
+        for u in range(WORD_HALVES):
+            row_first = HALF + u * PAIR * P
+            nc.sync.dma_start(
+                out=w_rows[:, PAIR * u : PAIR * (u + 1), :],
+                in_=target_matrix[row_first : row_first + PAIR * P, HALF:DIM].rearrange(
+                    "(p e) n -> p e n", e=PAIR
+                ),
+            )
+        state_sb = []
+        for c in range(CHUNKS):
+            state_chunk = resident.tile([P, CHUNK, DIM], BF16)
+            nc.sync.dma_start(
+                out=state_chunk[:], in_=state_rows[:, c * CHUNK : (c + 1) * CHUNK, :]
+            )
+            state_sb.append(state_chunk)
+
+        ident = const.tile([P, P], F32)
+        make_identity(nc, ident[:])
+
+        w_grouped = const.tile([P, HALF, PACK], BF16, align_bytes=64)
+        nc.vector.tensor_copy(out=w_grouped[:], in_=w_rows[:].rearrange("p t n -> p n t"))
+        w_codes = const.tile([P, HALF], U32, align_bytes=64)
+        w_scales = const.tile([P, HALF], U8, align_bytes=64)
+        nc.vector.quantize_mx(
+            out=w_codes[:].bitcast(FP8X4),
+            scales=w_scales[:],
+            in_=w_grouped[:].rearrange("p n t -> p (n t)"),
+        )
+
+        def transpose_chunk(c):
+            banks = []
+            for b in range(BANKS_PER_CHUNK):
+                words_t = psum_words.tile([P, GROUPS_PER_BANK, WORD_HALVES, P], F32)
+                for g in range(GROUPS_PER_BANK):
+                    words = state_sb[c][:, b * GROUPS_PER_BANK + g, HALF:DIM].bitcast(F32)
+                    for u in range(WORD_HALVES):
+                        nc.tensor.transpose(
+                            words_t[:, g, u, :], words[:, u * P : (u + 1) * P], ident[:]
+                        )
+                banks.append(words_t)
+            return banks
+
+        def finish_chunk(c, banks):
+            out_chunk = results.tile([P, CHUNK, DIM], F32)
+
+            grouped = stage.tile([P, CHUNK * P * PACK], BF16, align_bytes=64)
+            grouped_words = grouped[:].bitcast(F32).rearrange(
+                "p (g m u) -> p g m u", m=P, u=WORD_HALVES
+            )
+            for b in range(BANKS_PER_CHUNK):
+                nc.vector.tensor_copy(
+                    out=grouped_words[:, b * GROUPS_PER_BANK : (b + 1) * GROUPS_PER_BANK, :, :],
+                    in_=banks[b][:].rearrange("p g u m -> p g m u"),
+                )
+            nc.vector.tensor_copy(out=out_chunk[:, :, 0:HALF], in_=state_sb[c][:, :, 0:HALF])
+            codes = stage.tile([P, CHUNK * P], U32, align_bytes=64)
+            scales = stage.tile([P, CHUNK * P], U8, align_bytes=64)
+            nc.vector.quantize_mx(out=codes[:].bitcast(FP8X4), scales=scales[:], in_=grouped[:])
+
+            for g in range(CHUNK):
+                m_cols = slice(g * P, (g + 1) * P)
+                prod = psum_prod.tile([P, HALF], F32)
+                nc.tensor.matmul_mx(
+                    out=prod[:],
+                    lhsT=codes[:, m_cols].bitcast(FP8X4),
+                    lhsT_scale=scales[:, m_cols],
+                    rhs=w_codes[:].bitcast(FP8X4),
+                    rhs_scale=w_scales[:],
+                    start=True,
+                    stop=True,
+                )
+                nc.scalar.copy(out=out_chunk[:, g, HALF:DIM], in_=prod[:])
+
+            nc.sync.dma_start(out=out_rows[:, c * CHUNK : (c + 1) * CHUNK, :], in_=out_chunk[:])
+
+        banks_next = transpose_chunk(0)
+        for c in range(CHUNKS):
+            banks_now = banks_next
+            if c + 1 < CHUNKS:
+                banks_next = transpose_chunk(c + 1)
+            finish_chunk(c, banks_now)

@@ -19,14 +19,16 @@ WORD_HALVES = 2
 BANK_F32 = 512
 
 ROW_GROUPS = BATCH // P
-CHUNK = 4
+CHUNK = 8
 CHUNKS = ROW_GROUPS // CHUNK
+STEP = 4
+STEPS = ROW_GROUPS // STEP
+STEPS_PER_CHUNK = CHUNK // STEP
 GROUPS_PER_BANK = BANK_F32 // (WORD_HALVES * P)
-BANKS_PER_CHUNK = CHUNK // GROUPS_PER_BANK
+BANKS_PER_STEP = STEP // GROUPS_PER_BANK
 
-WORD_BANKS = 2 * BANKS_PER_CHUNK
+WORD_BANKS = 2 * BANKS_PER_STEP
 PROD_BANKS = 8 - WORD_BANKS
-OUT_BUFS = 4
 STAGE_BUFS = 3
 
 FLOPS = 2 * BATCH * HALF * HALF
@@ -45,7 +47,7 @@ def tile_builtcontrolled_t_kernel(tc, state, target_matrix, control, num_qubits,
         const = ctx.enter_context(tc.tile_pool(name="const", bufs=1))
         resident = ctx.enter_context(tc.tile_pool(name="resident", bufs=CHUNKS))
         stage = ctx.enter_context(tc.tile_pool(name="stage", bufs=STAGE_BUFS))
-        results = ctx.enter_context(tc.tile_pool(name="results", bufs=OUT_BUFS))
+        results = ctx.enter_context(tc.tile_pool(name="results", bufs=CHUNKS))
         psum_words = ctx.enter_context(tc.psum_pool(name="psum_words", bufs=WORD_BANKS))
         psum_prod = ctx.enter_context(tc.psum_pool(name="psum_prod", bufs=PROD_BANKS))
 
@@ -70,21 +72,23 @@ def tile_builtcontrolled_t_kernel(tc, state, target_matrix, control, num_qubits,
         make_identity(nc, ident[:])
 
         w_grouped = const.tile([P, HALF, PACK], BF16, align_bytes=64)
-        nc.vector.tensor_copy(out=w_grouped[:], in_=w_rows[:].rearrange("p t n -> p n t"))
+        nc.vector.tensor_copy(out=w_grouped[:], in_=w_rows[:].rearrange("p j n -> p n j"))
         w_codes = const.tile([P, HALF], U32, align_bytes=64)
         w_scales = const.tile([P, HALF], U8, align_bytes=64)
         nc.vector.quantize_mx(
             out=w_codes[:].bitcast(FP8X4),
             scales=w_scales[:],
-            in_=w_grouped[:].rearrange("p n t -> p (n t)"),
+            in_=w_grouped[:].rearrange("p n j -> p (n j)"),
         )
 
-        def transpose_chunk(c):
+        def transpose_step(s):
+            c, first = s // STEPS_PER_CHUNK, (s % STEPS_PER_CHUNK) * STEP
             banks = []
-            for b in range(BANKS_PER_CHUNK):
+            for b in range(BANKS_PER_STEP):
                 words_t = psum_words.tile([P, GROUPS_PER_BANK, WORD_HALVES, P], F32)
                 for g in range(GROUPS_PER_BANK):
-                    words = state_sb[c][:, b * GROUPS_PER_BANK + g, HALF:DIM].bitcast(F32)
+                    t = first + b * GROUPS_PER_BANK + g
+                    words = state_sb[c][:, t, HALF:DIM].bitcast(F32)
                     for u in range(WORD_HALVES):
                         nc.tensor.transpose(
                             words_t[:, g, u, :], words[:, u * P : (u + 1) * P], ident[:]
@@ -92,24 +96,27 @@ def tile_builtcontrolled_t_kernel(tc, state, target_matrix, control, num_qubits,
                 banks.append(words_t)
             return banks
 
-        def finish_chunk(c, banks):
-            out_chunk = results.tile([P, CHUNK, DIM], F32)
+        def finish_step(s, banks, out_chunk):
+            c, first = s // STEPS_PER_CHUNK, (s % STEPS_PER_CHUNK) * STEP
 
-            grouped = stage.tile([P, CHUNK * P * PACK], BF16, align_bytes=64)
+            grouped = stage.tile([P, STEP * P * PACK], BF16, align_bytes=64)
             grouped_words = grouped[:].bitcast(F32).rearrange(
                 "p (g m u) -> p g m u", m=P, u=WORD_HALVES
             )
-            for b in range(BANKS_PER_CHUNK):
+            for b in range(BANKS_PER_STEP):
                 nc.vector.tensor_copy(
                     out=grouped_words[:, b * GROUPS_PER_BANK : (b + 1) * GROUPS_PER_BANK, :, :],
                     in_=banks[b][:].rearrange("p g u m -> p g m u"),
                 )
-            nc.vector.tensor_copy(out=out_chunk[:, :, 0:HALF], in_=state_sb[c][:, :, 0:HALF])
-            codes = stage.tile([P, CHUNK * P], U32, align_bytes=64)
-            scales = stage.tile([P, CHUNK * P], U8, align_bytes=64)
+            nc.vector.tensor_copy(
+                out=out_chunk[:, first : first + STEP, 0:HALF],
+                in_=state_sb[c][:, first : first + STEP, 0:HALF],
+            )
+            codes = stage.tile([P, STEP * P], U32, align_bytes=64)
+            scales = stage.tile([P, STEP * P], U8, align_bytes=64)
             nc.vector.quantize_mx(out=codes[:].bitcast(FP8X4), scales=scales[:], in_=grouped[:])
 
-            for g in range(CHUNK):
+            for g in range(STEP):
                 m_cols = slice(g * P, (g + 1) * P)
                 prod = psum_prod.tile([P, HALF], F32)
                 nc.tensor.matmul_mx(
@@ -121,13 +128,14 @@ def tile_builtcontrolled_t_kernel(tc, state, target_matrix, control, num_qubits,
                     start=True,
                     stop=True,
                 )
-                nc.scalar.copy(out=out_chunk[:, g, HALF:DIM], in_=prod[:])
+                nc.scalar.copy(out=out_chunk[:, first + g, HALF:DIM], in_=prod[:])
 
-            nc.sync.dma_start(out=out_rows[:, c * CHUNK : (c + 1) * CHUNK, :], in_=out_chunk[:])
-
-        banks_next = transpose_chunk(0)
+        banks_next = transpose_step(0)
         for c in range(CHUNKS):
-            banks_now = banks_next
-            if c + 1 < CHUNKS:
-                banks_next = transpose_chunk(c + 1)
-            finish_chunk(c, banks_now)
+            out_chunk = results.tile([P, CHUNK, DIM], F32)
+            for s in range(c * STEPS_PER_CHUNK, (c + 1) * STEPS_PER_CHUNK):
+                banks_now = banks_next
+                if s + 1 < STEPS:
+                    banks_next = transpose_step(s + 1)
+                finish_step(s, banks_now, out_chunk)
+            nc.sync.dma_start(out=out_rows[:, c * CHUNK : (c + 1) * CHUNK, :], in_=out_chunk[:])

@@ -40,8 +40,8 @@ def tile_builtcontrolled_t_kernel(tc, state, target_matrix, control, num_qubits,
     assert control == 0 and num_qubits == 10
     assert tuple(state.shape) == (BATCH, DIM) and tuple(target_matrix.shape) == (DIM, DIM)
 
-    state_rows = state.rearrange("(p t) d -> p t d", t=ROW_GROUPS)
-    out_rows = out.rearrange("(p t) d -> p t d", t=ROW_GROUPS)
+    state_rows = state.rearrange("(c p t) d -> c p t d", p=P, t=CHUNK)
+    out_rows = out.rearrange("(c p t) d -> c p t d", p=P, t=CHUNK)
 
     with ExitStack() as ctx:
         const = ctx.enter_context(tc.tile_pool(name="const", bufs=1))
@@ -64,7 +64,7 @@ def tile_builtcontrolled_t_kernel(tc, state, target_matrix, control, num_qubits,
         for c in range(CHUNKS):
             state_chunk = resident.tile([P, CHUNK, DIM], BF16)
             nc.sync.dma_start(
-                out=state_chunk[:], in_=state_rows[:, c * CHUNK : (c + 1) * CHUNK, :]
+                out=state_chunk[:], in_=state_rows[c]
             )
             state_sb.append(state_chunk)
 
@@ -138,4 +138,4 @@ def tile_builtcontrolled_t_kernel(tc, state, target_matrix, control, num_qubits,
                 if s + 1 < STEPS:
                     banks_next = transpose_step(s + 1)
                 finish_step(s, banks_now, out_chunk)
-            nc.sync.dma_start(out=out_rows[:, c * CHUNK : (c + 1) * CHUNK, :], in_=out_chunk[:])
+            nc.sync.dma_start(out=out_rows[c], in_=out_chunk[:])

@@ -51,7 +51,7 @@ def tile_builtcontrolled_t_kernel(tc, state, target_matrix, control, num_qubits,
         psum_words = ctx.enter_context(tc.psum_pool(name="psum_words", bufs=WORD_BANKS))
         psum_prod = ctx.enter_context(tc.psum_pool(name="psum_prod", bufs=PROD_BANKS))
 
-        w_rows = const.tile([P, PACK, HALF], BF16)
+        w_rows = const.tile([P, PACK, HALF], BF16, align_bytes=512)
         for u in range(WORD_HALVES):
             row_first = HALF + u * PAIR * P
             nc.sync.dma_start(
@@ -62,7 +62,7 @@ def tile_builtcontrolled_t_kernel(tc, state, target_matrix, control, num_qubits,
             )
         state_sb = []
         for c in range(CHUNKS):
-            state_chunk = resident.tile([P, CHUNK, DIM], BF16)
+            state_chunk = resident.tile([P, CHUNK, DIM], BF16, align_bytes=512)
             nc.sync.dma_start(
                 out=state_chunk[:], in_=state_rows[c]
             )
@@ -132,7 +132,7 @@ def tile_builtcontrolled_t_kernel(tc, state, target_matrix, control, num_qubits,
 
         banks_next = transpose_step(0)
         for c in range(CHUNKS):
-            out_chunk = results.tile([P, CHUNK, DIM], F32)
+            out_chunk = results.tile([P, CHUNK, DIM], F32, align_bytes=512)
             for s in range(c * STEPS_PER_CHUNK, (c + 1) * STEPS_PER_CHUNK):
                 banks_now = banks_next
                 if s + 1 < STEPS:

@@ -19,11 +19,9 @@ WORD_HALVES = 2
 BANK_F32 = 512
 
 ROW_GROUPS = BATCH // P
-CHUNK = 8
-CHUNKS = ROW_GROUPS // CHUNK
+CHUNK_GROUPS = (8, 8, 16)
 STEP = 4
 STEPS = ROW_GROUPS // STEP
-STEPS_PER_CHUNK = CHUNK // STEP
 GROUPS_PER_BANK = BANK_F32 // (WORD_HALVES * P)
 BANKS_PER_STEP = STEP // GROUPS_PER_BANK
 
@@ -40,14 +38,16 @@ def tile_builtcontrolled_t_kernel(tc, state, target_matrix, control, num_qubits,
     assert control == 0 and num_qubits == 10
     assert tuple(state.shape) == (BATCH, DIM) and tuple(target_matrix.shape) == (DIM, DIM)
 
-    state_rows = state.rearrange("(c p t) d -> c p t d", p=P, t=CHUNK)
-    out_rows = out.rearrange("(c p t) d -> c p t d", p=P, t=CHUNK)
+    def chunk_rows(tensor, c):
+        row_first = P * sum(CHUNK_GROUPS[:c])
+        rows = tensor[row_first : row_first + P * CHUNK_GROUPS[c], :]
+        return rows.rearrange("(p t) d -> p t d", p=P)
 
     with ExitStack() as ctx:
         const = ctx.enter_context(tc.tile_pool(name="const", bufs=1))
-        resident = ctx.enter_context(tc.tile_pool(name="resident", bufs=CHUNKS))
+        resident = ctx.enter_context(tc.tile_pool(name="resident", bufs=1))
         stage = ctx.enter_context(tc.tile_pool(name="stage", bufs=STAGE_BUFS))
-        results = ctx.enter_context(tc.tile_pool(name="results", bufs=CHUNKS))
+        results = ctx.enter_context(tc.tile_pool(name="results", bufs=1))
         psum_words = ctx.enter_context(tc.psum_pool(name="psum_words", bufs=WORD_BANKS))
         psum_prod = ctx.enter_context(tc.psum_pool(name="psum_prod", bufs=PROD_BANKS))
 
@@ -60,13 +60,14 @@ def tile_builtcontrolled_t_kernel(tc, state, target_matrix, control, num_qubits,
                     "(p e) n -> p e n", e=PAIR
                 ),
             )
-        state_sb = []
-        for c in range(CHUNKS):
-            state_chunk = resident.tile([P, CHUNK, DIM], BF16, align_bytes=512)
-            nc.sync.dma_start(
-                out=state_chunk[:], in_=state_rows[c]
+        step_place = []
+        for c, groups in enumerate(CHUNK_GROUPS):
+            state_chunk = resident.tile(
+                [P, groups, DIM], BF16, name="state_%d" % c, align_bytes=512
             )
-            state_sb.append(state_chunk)
+            nc.sync.dma_start(out=state_chunk[:], in_=chunk_rows(state, c))
+            for first in range(0, groups, STEP):
+                step_place.append((state_chunk, first))
 
         ident = const.tile([P, P], F32)
         make_identity(nc, ident[:])
@@ -82,13 +83,13 @@ def tile_builtcontrolled_t_kernel(tc, state, target_matrix, control, num_qubits,
         )
 
         def transpose_step(s):
-            c, first = s // STEPS_PER_CHUNK, (s % STEPS_PER_CHUNK) * STEP
+            state_chunk, first = step_place[s]
             banks = []
             for b in range(BANKS_PER_STEP):
                 words_t = psum_words.tile([P, GROUPS_PER_BANK, WORD_HALVES, P], F32)
                 for g in range(GROUPS_PER_BANK):
                     t = first + b * GROUPS_PER_BANK + g
-                    words = state_sb[c][:, t, HALF:DIM].bitcast(F32)
+                    words = state_chunk[:, t, HALF:DIM].bitcast(F32)
                     for u in range(WORD_HALVES):
                         nc.tensor.transpose(
                             words_t[:, g, u, :], words[:, u * P : (u + 1) * P], ident[:]
@@ -97,7 +98,7 @@ def tile_builtcontrolled_t_kernel(tc, state, target_matrix, control, num_qubits,
             return banks
 
         def finish_step(s, banks, out_chunk):
-            c, first = s // STEPS_PER_CHUNK, (s % STEPS_PER_CHUNK) * STEP
+            state_chunk, first = step_place[s]
 
             grouped = stage.tile([P, STEP * P * PACK], BF16, align_bytes=64)
             grouped_words = grouped[:].bitcast(F32).rearrange(
@@ -110,7 +111,7 @@ def tile_builtcontrolled_t_kernel(tc, state, target_matrix, control, num_qubits,
                 )
             nc.vector.tensor_copy(
                 out=out_chunk[:, first : first + STEP, 0:HALF],
-                in_=state_sb[c][:, first : first + STEP, 0:HALF],
+                in_=state_chunk[:, first : first + STEP, 0:HALF],
             )
             codes = stage.tile([P, STEP * P], U32, align_bytes=64)
             scales = stage.tile([P, STEP * P], U8, align_bytes=64)
@@ -131,11 +132,13 @@ def tile_builtcontrolled_t_kernel(tc, state, target_matrix, control, num_qubits,
                 nc.scalar.copy(out=out_chunk[:, first + g, HALF:DIM], in_=prod[:])
 
         banks_next = transpose_step(0)
-        for c in range(CHUNKS):
-            out_chunk = results.tile([P, CHUNK, DIM], F32, align_bytes=512)
-            for s in range(c * STEPS_PER_CHUNK, (c + 1) * STEPS_PER_CHUNK):
+        s = 0
+        for c, groups in enumerate(CHUNK_GROUPS):
+            out_chunk = results.tile([P, groups, DIM], F32, name="out_%d" % c, align_bytes=512)
+            for step_of_chunk in range(groups // STEP):
                 banks_now = banks_next
                 if s + 1 < STEPS:
                     banks_next = transpose_step(s + 1)
                 finish_step(s, banks_now, out_chunk)
-            nc.sync.dma_start(out=out_rows[c], in_=out_chunk[:])
+                s += 1
+            nc.sync.dma_start(out=chunk_rows(out, c), in_=out_chunk[:])

@@ -50,6 +50,7 @@ def tile_builtcontrolled_t_kernel(tc, state, target_matrix, control, num_qubits,
         results = ctx.enter_context(tc.tile_pool(name="results", bufs=1))
         psum_words = ctx.enter_context(tc.psum_pool(name="psum_words", bufs=WORD_BANKS))
         psum_prod = ctx.enter_context(tc.psum_pool(name="psum_prod", bufs=PROD_BANKS))
+        ctx.enter_context(tc.manual_schedule(engines={mybir.EngineType.DVE}))
 
         w_rows = const.tile([P, PACK, HALF], BF16, align_bytes=512)
         for u in range(WORD_HALVES):
@@ -60,12 +61,14 @@ def tile_builtcontrolled_t_kernel(tc, state, target_matrix, control, num_qubits,
                     "(p e) n -> p e n", e=PAIR
                 ),
             )
+        state_sb = []
         step_place = []
         for c, groups in enumerate(CHUNK_GROUPS):
             state_chunk = resident.tile(
                 [P, groups, DIM], BF16, name="state_%d" % c, align_bytes=512
             )
             nc.sync.dma_start(out=state_chunk[:], in_=chunk_rows(state, c))
+            state_sb.append(state_chunk)
             for first in range(0, groups, STEP):
                 step_place.append((state_chunk, first))
 
@@ -98,7 +101,7 @@ def tile_builtcontrolled_t_kernel(tc, state, target_matrix, control, num_qubits,
             return banks
 
         def finish_step(s, banks, out_chunk):
-            state_chunk, first = step_place[s]
+            first = step_place[s][1]
 
             grouped = stage.tile([P, STEP * P * PACK], BF16, align_bytes=64)
             grouped_words = grouped[:].bitcast(F32).rearrange(
@@ -109,10 +112,6 @@ def tile_builtcontrolled_t_kernel(tc, state, target_matrix, control, num_qubits,
                     out=grouped_words[:, b * GROUPS_PER_BANK : (b + 1) * GROUPS_PER_BANK, :, :],
                     in_=banks[b][:].rearrange("p g u m -> p g m u"),
                 )
-            nc.vector.tensor_copy(
-                out=out_chunk[:, first : first + STEP, 0:HALF],
-                in_=state_chunk[:, first : first + STEP, 0:HALF],
-            )
             codes = stage.tile([P, STEP * P], U32, align_bytes=64)
             scales = stage.tile([P, STEP * P], U8, align_bytes=64)
             nc.vector.quantize_mx(out=codes[:].bitcast(FP8X4), scales=scales[:], in_=grouped[:])
@@ -141,4 +140,5 @@ def tile_builtcontrolled_t_kernel(tc, state, target_matrix, control, num_qubits,
                     banks_next = transpose_step(s + 1)
                 finish_step(s, banks_now, out_chunk)
                 s += 1
+            nc.vector.tensor_copy(out=out_chunk[:, :, 0:HALF], in_=state_sb[c][:, :, 0:HALF])
             nc.sync.dma_start(out=chunk_rows(out, c), in_=out_chunk[:])

from contextlib import ExitStack

import concourse.mybir as mybir
from concourse.masks import make_identity

BF16 = mybir.dt.bfloat16
F32 = mybir.dt.float32
U32 = mybir.dt.uint32
U8 = mybir.dt.uint8
FP8X4 = mybir.dt.float8_e4m3fn_x4

P = 128
PACK = 4
BATCH = 4096
DIM = 1024
HALF = DIM // 2
PAIR = 2
WORD_HALVES = 2
BANK_F32 = 512

ROW_GROUPS = BATCH // P
CHUNK_GROUPS = (8, 8, 16)
STEP = 4
STEPS = ROW_GROUPS // STEP
GROUPS_PER_BANK = BANK_F32 // (WORD_HALVES * P)
BANKS_PER_STEP = STEP // GROUPS_PER_BANK

WORD_BANKS = 2 * BANKS_PER_STEP
PROD_BANKS = 8 - WORD_BANKS
STAGE_BUFS = 3

FLOPS = 2 * BATCH * HALF * HALF
BYTES = BATCH * DIM * 2 + HALF * HALF * 2 + BATCH * DIM * 4


def tile_builtcontrolled_t_kernel(tc, state, target_matrix, control, num_qubits, out):
    nc = tc.nc
    assert control == 0 and num_qubits == 10
    assert tuple(state.shape) == (BATCH, DIM) and tuple(target_matrix.shape) == (DIM, DIM)

    def chunk_rows(tensor, c):
        row_first = P * sum(CHUNK_GROUPS[:c])
        rows = tensor[row_first : row_first + P * CHUNK_GROUPS[c], :]
        return rows.rearrange("(p t) d -> p t d", p=P)

    with ExitStack() as ctx:
        const = ctx.enter_context(tc.tile_pool(name="const", bufs=1))
        resident = ctx.enter_context(tc.tile_pool(name="resident", bufs=1))
        stage = ctx.enter_context(tc.tile_pool(name="stage", bufs=STAGE_BUFS))
        results = ctx.enter_context(tc.tile_pool(name="results", bufs=1))
        psum_words = ctx.enter_context(tc.psum_pool(name="psum_words", bufs=WORD_BANKS))
        psum_prod = ctx.enter_context(tc.psum_pool(name="psum_prod", bufs=PROD_BANKS))
        ctx.enter_context(tc.manual_schedule(engines={mybir.EngineType.DVE}))

        w_rows = const.tile([P, PACK, HALF], BF16, align_bytes=512)
        for u in range(WORD_HALVES):
            row_first = HALF + u * PAIR * P
            nc.sync.dma_start(
                out=w_rows[:, PAIR * u : PAIR * (u + 1), :],
                in_=target_matrix[row_first : row_first + PAIR * P, HALF:DIM].rearrange(
                    "(p e) n -> p e n", e=PAIR
                ),
            )
        state_sb = []
        step_place = []
        for c, groups in enumerate(CHUNK_GROUPS):
            state_chunk = resident.tile(
                [P, groups, DIM], BF16, name="state_%d" % c, align_bytes=512
            )
            nc.sync.dma_start(out=state_chunk[:], in_=chunk_rows(state, c))
            state_sb.append(state_chunk)
            for first in range(0, groups, STEP):
                step_place.append((state_chunk, first))

        ident = const.tile([P, P], F32)
        make_identity(nc, ident[:])

        w_grouped = const.tile([P, HALF, PACK], BF16, align_bytes=64)
        nc.vector.tensor_copy(out=w_grouped[:], in_=w_rows[:].rearrange("p j n -> p n j"))
        w_codes = const.tile([P, HALF], U32, align_bytes=64)
        w_scales = const.tile([P, HALF], U8, align_bytes=64)
        nc.vector.quantize_mx(
            out=w_codes[:].bitcast(FP8X4),
            scales=w_scales[:],
            in_=w_grouped[:].rearrange("p n j -> p (n j)"),
        )

        def transpose_step(s):
            state_chunk, first = step_place[s]
            banks = []
            for b in range(BANKS_PER_STEP):
                words_t = psum_words.tile([P, GROUPS_PER_BANK, WORD_HALVES, P], F32)
                for g in range(GROUPS_PER_BANK):
                    t = first + b * GROUPS_PER_BANK + g
                    words = state_chunk[:, t, HALF:DIM].bitcast(F32)
                    for u in range(WORD_HALVES):
                        nc.tensor.transpose(
                            words_t[:, g, u, :], words[:, u * P : (u + 1) * P], ident[:]
                        )
                banks.append(words_t)
            return banks

        def finish_step(s, banks, out_chunk):
            first = step_place[s][1]

            grouped = stage.tile([P, STEP * P * PACK], BF16, align_bytes=64)
            grouped_words = grouped[:].bitcast(F32).rearrange(
                "p (g m u) -> p g m u", m=P, u=WORD_HALVES
            )
            for b in range(BANKS_PER_STEP):
                nc.vector.tensor_copy(
                    out=grouped_words[:, b * GROUPS_PER_BANK : (b + 1) * GROUPS_PER_BANK, :, :],
                    in_=banks[b][:].rearrange("p g u m -> p g m u"),
                )
            codes = stage.tile([P, STEP * P], U32, align_bytes=64)
            scales = stage.tile([P, STEP * P], U8, align_bytes=64)
            nc.vector.quantize_mx(out=codes[:].bitcast(FP8X4), scales=scales[:], in_=grouped[:])

            for g in range(STEP):
                m_cols = slice(g * P, (g + 1) * P)
                prod = psum_prod.tile([P, HALF], F32)
                nc.tensor.matmul_mx(
                    out=prod[:],
                    lhsT=codes[:, m_cols].bitcast(FP8X4),
                    lhsT_scale=scales[:, m_cols],
                    rhs=w_codes[:].bitcast(FP8X4),
                    rhs_scale=w_scales[:],
                    start=True,
                    stop=True,
                )
                nc.scalar.copy(out=out_chunk[:, first + g, HALF:DIM], in_=prod[:])

        banks_next = transpose_step(0)
        s = 0
        for c, groups in enumerate(CHUNK_GROUPS):
            out_chunk = results.tile([P, groups, DIM], F32, name="out_%d" % c, align_bytes=512)
            for step_of_chunk in range(groups // STEP):
                banks_now = banks_next
                if s + 1 < STEPS:
                    banks_next = transpose_step(s + 1)
                finish_step(s, banks_now, out_chunk)
                s += 1
            nc.vector.tensor_copy(out=out_chunk[:, :, 0:HALF], in_=state_sb[c][:, :, 0:HALF])
            nc.sync.dma_start(out=chunk_rows(out, c), in_=out_chunk[:])
